import numpy as np
import ml_dtypes


def mxq(x, axis, fmt="e4m3"):
    dtype, down = {"e4m3": (ml_dtypes.float8_e4m3fn, 7), "e5m2": (ml_dtypes.float8_e5m2, 14)}[fmt]
    v = np.moveaxis(np.asarray(x, np.float32).astype(ml_dtypes.bfloat16).astype(np.float64), axis, -1)
    blocks = v.reshape(v.shape[:-1] + (-1, 32))
    amax = np.abs(blocks).max(-1, keepdims=True)
    byte = np.maximum(np.where(amax > 0, np.frexp(amax)[1] - 1 + 127, 0) - down, 1)
    scale = np.exp2(byte - 127.0)
    codes = (blocks / scale).astype(np.float32).astype(dtype).astype(np.float64)
    return np.moveaxis((codes * scale).reshape(v.shape), -1, axis)


WIDE = False


def mx_kscale(k):
    if not WIDE:
        return np.ones(k)
    levels = np.array([10, -10, 5, -5, 0])
    if k % 512:
        return np.exp2(np.random.permutation(np.resize(levels, k // 32))).repeat(32)
    a = np.empty((k // 512, 16))
    for p in range(k // 512):
        a[p, :8] = np.random.permutation(np.resize(levels, 8))
        for g in range(8):
            far = levels[np.abs(levels - a[p, g]) >= 10]
            a[p, g + 8] = far[np.random.randint(len(far))]
    return np.exp2(a.ravel()).repeat(32)


BF16 = ml_dtypes.bfloat16


def bf(x):
    return np.asarray(x, np.float32).astype(BF16)


def f64(x):
    return np.asarray(x).astype(np.float64)


B, S, D, H, DH, DV, R = 4, 256, 2048, 16, 128, 128, 512
ROPE_THETA = 10000.0


def apply_rope(t, cos, sin):
    b, s, h, d = t.shape
    tr = t.reshape(b, s, h, d // 2, 2)
    x1, x2 = tr[..., 0], tr[..., 1]
    c = cos[None, :, None, :]
    sn = sin[None, :, None, :]
    o1 = x1 * c - x2 * sn
    o2 = x1 * sn + x2 * c
    return np.stack([o1, o2], axis=-1).reshape(b, s, h, d)


def setup_inputs():
    s = mx_kscale(D)
    inv_freq = 1.0 / ROPE_THETA ** (np.arange(0, DH, 2) / DH)
    ang = np.arange(S)[:, None] * inv_freq[None, :]
    return {"x": bf(np.random.standard_normal((B, S, D)) * s),
            "freqs_cos": bf(np.cos(ang)),
            "freqs_sin": bf(np.sin(ang)),
            "w_q": bf(np.random.standard_normal((D, H * DH)) / np.sqrt(D) / s[:, None])}


def reference(x, freqs_cos, freqs_sin, w_q):
    q = (mxq(f64(x), 2, "e4m3") @ mxq(f64(w_q), 0, "e4m3")).reshape(B, S, H, DH)
    return apply_rope(q, f64(freqs_cos), f64(freqs_sin))

@@ -1,0 +1,184 @@
+import concourse.mybir as mybir
+from concourse.masks import make_identity
+
+F32 = mybir.dt.float32
+BF16 = mybir.dt.bfloat16
+U32 = mybir.dt.uint32
+U8 = mybir.dt.uint8
+FP8X4 = mybir.dt.float8_e4m3fn_x4
+MULT = mybir.AluOpType.mult
+ADD = mybir.AluOpType.add
+
+P = 128
+PACK = 4
+K_PASS = P * PACK
+TOKENS = 4 * 256
+SEQ = 256
+D_IN = 2048
+D_OUT = 2048
+HEAD = 128
+PAIRS = HEAD // 2
+PASSES = D_IN // K_PASS
+TOKEN_TILES = TOKENS // P
+SEQ_TILES = SEQ // P
+CHUNK = 512
+CHUNKS = D_OUT // CHUNK
+CHUNK_HEADS = CHUNK // HEAD
+
+FLOPS = 2 * TOKENS * D_IN * D_OUT
+
+
+def tile_mla_pb_kernel(tc, x, freqs_cos, freqs_sin, w_q, out):
+    nc = tc.nc
+    x_rows = x.flatten_outer_dims()
+    out_rows = out.rearrange("b s h d -> (b s) (h d)")
+
+    with (
+        tc.tile_pool(name="const", bufs=1) as const,
+        tc.tile_pool(name="x_in", bufs=4) as x_in,
+        tc.tile_pool(name="w_in", bufs=3) as w_in,
+        tc.tile_pool(name="x_stage", bufs=2) as x_stage,
+        tc.tile_pool(name="w_stage", bufs=4) as w_stage,
+        tc.tile_pool(name="w_mx", bufs=3) as w_mx,
+        tc.tile_pool(name="products", bufs=4) as products,
+        tc.tile_pool(name="results", bufs=12) as results,
+        tc.psum_pool(name="banks", bufs=8) as banks,
+    ):
+        ident = const.tile([P, P], F32)
+        make_identity(nc, ident[:])
+
+        cos_rows = const.tile([P, SEQ_TILES, PAIRS], BF16)
+        sin_rows = const.tile([P, SEQ_TILES, PAIRS], BF16)
+        nc.scalar.dma_start(out=cos_rows[:], in_=freqs_cos.rearrange("(t p) i -> p t i", p=P))
+        nc.scalar.dma_start(out=sin_rows[:], in_=freqs_sin.rearrange("(t p) i -> p t i", p=P))
+        table_even = const.tile([P, SEQ_TILES, PAIRS, 2], BF16)
+        table_odd = const.tile([P, SEQ_TILES, PAIRS, 2], BF16)
+        nc.vector.tensor_copy(out=table_even[:, :, :, 0], in_=cos_rows[:])
+        nc.vector.tensor_copy(out=table_even[:, :, :, 1], in_=sin_rows[:])
+        nc.vector.tensor_scalar_mul(out=table_odd[:, :, :, 0], in0=sin_rows[:], scalar1=-1.0)
+        nc.vector.tensor_copy(out=table_odd[:, :, :, 1], in_=cos_rows[:])
+
+        x_codes = const.tile([P, TOKEN_TILES, PASSES * P], U32, align_bytes=64)
+        x_scales = const.tile([P, TOKEN_TILES, PASSES * P], U8, align_bytes=64)
+
+        x_raw_tiles = {}
+        w_raw_tiles = {}
+        w_code_tiles = {}
+        w_scale_tiles = {}
+        w_grouped_tiles = {}
+
+        def load_x(m):
+            x_raw = x_in.tile([P, D_IN], BF16, name="x_raw")
+            nc.sync.dma_start(out=x_raw[:], in_=x_rows[m * P : (m + 1) * P, :])
+            x_raw_tiles[m] = x_raw
+
+        def load_w(c):
+            w_raw = w_in.tile([P, PASSES, PACK, CHUNK], BF16, name="w_raw")
+            for g in range(PASSES):
+                nc.sync.dma_start(
+                    out=w_raw[:, g],
+                    in_=w_q[
+                        g * K_PASS : (g + 1) * K_PASS, c * CHUNK : (c + 1) * CHUNK
+                    ].rearrange("(p t) n -> p t n", t=PACK),
+                )
+            w_raw_tiles[c] = w_raw
+            w_code_tiles[c] = w_mx.tile([P, PASSES, CHUNK], U32, name="w_codes", align_bytes=64)
+            w_scale_tiles[c] = w_mx.tile([P, PASSES, CHUNK], U8, name="w_scales", align_bytes=64)
+
+        def prepare_x(m):
+            x_words = x_raw_tiles[m][:].bitcast(F32)
+            x_grouped = x_stage.tile([P, PASSES * P * PACK], BF16, align_bytes=64)
+            grouped_words = x_grouped[:].bitcast(F32).rearrange(
+                "p (g r u) -> p g r u", g=PASSES, u=2
+            )
+            for half in range(2):
+                x_t = banks.tile([P, 2, 2, P], F32, name="x_t", tag="bank")
+                for gl in range(2):
+                    for u in range(2):
+                        first = (2 * half + gl) * 2 * P
+                        nc.tensor.transpose(
+                            x_t[:, gl, u, :],
+                            x_words[:, first + u : first + 2 * P : 2],
+                            ident[:],
+                        )
+                nc.scalar.copy(
+                    out=grouped_words[:, 2 * half : 2 * half + 2],
+                    in_=x_t[:].rearrange("p g u r -> p g r u"),
+                )
+            nc.vector.quantize_mx(
+                out=x_codes[:, m, :].bitcast(FP8X4), scales=x_scales[:, m, :], in_=x_grouped[:]
+            )
+
+        def regroup_w(c, g, engine_copy):
+            w_grouped = w_stage.tile([P, CHUNK, PACK], BF16, name="w_grouped", align_bytes=64)
+            engine_copy(
+                out=w_grouped[:].rearrange("p (n i) t -> p n t i", i=4),
+                in_=w_raw_tiles[c][:, g].rearrange("p t (n i) -> p n t i", i=4),
+            )
+            w_grouped_tiles[(c, g)] = w_grouped
+
+        def quantise_w(c, g):
+            nc.vector.quantize_mx(
+                out=w_code_tiles[c][:, g, :].bitcast(FP8X4),
+                scales=w_scale_tiles[c][:, g, :],
+                in_=w_grouped_tiles[(c, g)][:].rearrange("p n t -> p (n t)"),
+            )
+
+        def project_and_rotate(c, m):
+            acc = banks.tile([P, CHUNK], F32, name="acc", tag="bank")
+            for g in range(PASSES):
+                nc.tensor.matmul_mx(
+                    out=acc[:],
+                    lhsT=x_codes[:, m, g * P : (g + 1) * P].bitcast(FP8X4),
+                    lhsT_scale=x_scales[:, m, g * P : (g + 1) * P],
+                    rhs=w_code_tiles[c][:, g, :].bitcast(FP8X4),
+                    rhs_scale=w_scale_tiles[c][:, g, :],
+                    start=(g == 0),
+                    stop=(g == PASSES - 1),
+                )
+            shape = [P, CHUNK_HEADS, PAIRS, 2]
+            pairs = acc[:].rearrange("p (h i e) -> p h i e", i=PAIRS, e=2)
+            t = m % SEQ_TILES
+            from_even = products.tile(shape, F32)
+            from_odd = products.tile(shape, F32)
+            nc.vector.tensor_tensor(
+                out=from_even[:],
+                in0=pairs[:, :, :, 0:1].to_broadcast(shape),
+                in1=table_even[:, t].unsqueeze(1).to_broadcast(shape),
+                op=MULT,
+            )
+            nc.vector.tensor_tensor(
+                out=from_odd[:],
+                in0=pairs[:, :, :, 1:2].to_broadcast(shape),
+                in1=table_odd[:, t].unsqueeze(1).to_broadcast(shape),
+                op=MULT,
+            )
+            rotated = results.tile(shape, F32)
+            nc.gpsimd.tensor_tensor(out=rotated[:], in0=from_even[:], in1=from_odd[:], op=ADD)
+            nc.sync.dma_start(
+                out=out_rows[m * P : (m + 1) * P, c * CHUNK : (c + 1) * CHUNK],
+                in_=rotated[:].rearrange("p h i e -> p (h i e)"),
+            )
+
+        load_x(0)
+        load_w(0)
+        for m in range(1, TOKEN_TILES):
+            load_x(m)
+        for c in range(1, CHUNKS):
+            load_w(c)
+
+        prepare_x(0)
+        regroup_w(0, 0, nc.vector.tensor_copy)
+        for g in range(1, PASSES):
+            regroup_w(0, g, nc.vector.tensor_copy)
+            quantise_w(0, g - 1)
+        quantise_w(0, PASSES - 1)
+
+        for c in range(CHUNKS):
+            for m in range(TOKEN_TILES):
+                if c == 0 and m + 1 < TOKEN_TILES:
+                    prepare_x(m + 1)
+                project_and_rotate(c, m)
+                if c + 1 < CHUNKS and m % 2 == 1:
+                    regroup_w(c + 1, m // 2, nc.scalar.copy)
+                    quantise_w(c + 1, m // 2)

@@ -13,14 +13,13 @@ P = 128
 PACK = 4
 K_PASS = P * PACK
 TOKENS = 4 * 256
-SEQ = 256
 D_IN = 2048
 D_OUT = 2048
 HEAD = 128
 PAIRS = HEAD // 2
 PASSES = D_IN // K_PASS
 TOKEN_TILES = TOKENS // P
-SEQ_TILES = SEQ // P
+SEQ_TILES = 256 // P
 CHUNK = 512
 CHUNKS = D_OUT // CHUNK
 CHUNK_HEADS = CHUNK // HEAD
@@ -35,36 +34,29 @@ def tile_mla_pb_kernel(tc, x, freqs_cos, freqs_sin, w_q, out):
 
     with (
         tc.tile_pool(name="const", bufs=1) as const,
-        tc.tile_pool(name="x_in", bufs=4) as x_in,
-        tc.tile_pool(name="w_in", bufs=3) as w_in,
-        tc.tile_pool(name="x_stage", bufs=2) as x_stage,
+        tc.tile_pool(name="x_in", bufs=TOKEN_TILES) as x_in,
+        tc.tile_pool(name="w_in", bufs=CHUNKS * PASSES) as w_in,
+        tc.tile_pool(name="x_stage", bufs=3) as x_stage,
         tc.tile_pool(name="w_stage", bufs=4) as w_stage,
-        tc.tile_pool(name="w_mx", bufs=3) as w_mx,
-        tc.tile_pool(name="products", bufs=4) as products,
-        tc.tile_pool(name="results", bufs=12) as results,
-        tc.psum_pool(name="banks", bufs=8) as banks,
+        tc.tile_pool(name="products", bufs=3) as products,
+        tc.tile_pool(name="results", bufs=6) as results,
+        tc.psum_pool(name="turned", bufs=4) as turned,
+        tc.psum_pool(name="sums", bufs=4) as sums,
+        tc.manual_schedule(),
     ):
         ident = const.tile([P, P], F32)
-        make_identity(nc, ident[:])
-
         cos_rows = const.tile([P, SEQ_TILES, PAIRS], BF16)
         sin_rows = const.tile([P, SEQ_TILES, PAIRS], BF16)
-        nc.scalar.dma_start(out=cos_rows[:], in_=freqs_cos.rearrange("(t p) i -> p t i", p=P))
-        nc.scalar.dma_start(out=sin_rows[:], in_=freqs_sin.rearrange("(t p) i -> p t i", p=P))
-        table_even = const.tile([P, SEQ_TILES, PAIRS, 2], BF16)
-        table_odd = const.tile([P, SEQ_TILES, PAIRS, 2], BF16)
-        nc.vector.tensor_copy(out=table_even[:, :, :, 0], in_=cos_rows[:])
-        nc.vector.tensor_copy(out=table_even[:, :, :, 1], in_=sin_rows[:])
-        nc.vector.tensor_scalar_mul(out=table_odd[:, :, :, 0], in0=sin_rows[:], scalar1=-1.0)
-        nc.vector.tensor_copy(out=table_odd[:, :, :, 1], in_=cos_rows[:])
-
+        table = const.tile([P, SEQ_TILES, 2, PAIRS, 2], BF16)
         x_codes = const.tile([P, TOKEN_TILES, PASSES * P], U32, align_bytes=64)
         x_scales = const.tile([P, TOKEN_TILES, PASSES * P], U8, align_bytes=64)
+        w_codes = const.tile([P, CHUNKS, PASSES, CHUNK], U32, align_bytes=64)
+        w_scales = const.tile([P, CHUNKS, PASSES, CHUNK], U8, align_bytes=64)
 
         x_raw_tiles = {}
+        x_turned_tiles = {}
+        x_grouped_tiles = {}
         w_raw_tiles = {}
-        w_code_tiles = {}
-        w_scale_tiles = {}
         w_grouped_tiles = {}
 
         def load_x(m):
@@ -72,27 +64,20 @@ def tile_mla_pb_kernel(tc, x, freqs_cos, freqs_sin, w_q, out):
             nc.sync.dma_start(out=x_raw[:], in_=x_rows[m * P : (m + 1) * P, :])
             x_raw_tiles[m] = x_raw
 
-        def load_w(c):
-            w_raw = w_in.tile([P, PASSES, PACK, CHUNK], BF16, name="w_raw")
-            for g in range(PASSES):
-                nc.sync.dma_start(
-                    out=w_raw[:, g],
-                    in_=w_q[
-                        g * K_PASS : (g + 1) * K_PASS, c * CHUNK : (c + 1) * CHUNK
-                    ].rearrange("(p t) n -> p t n", t=PACK),
-                )
-            w_raw_tiles[c] = w_raw
-            w_code_tiles[c] = w_mx.tile([P, PASSES, CHUNK], U32, name="w_codes", align_bytes=64)
-            w_scale_tiles[c] = w_mx.tile([P, PASSES, CHUNK], U8, name="w_scales", align_bytes=64)
-
-        def prepare_x(m):
-            x_words = x_raw_tiles[m][:].bitcast(F32)
-            x_grouped = x_stage.tile([P, PASSES * P * PACK], BF16, align_bytes=64)
-            grouped_words = x_grouped[:].bitcast(F32).rearrange(
-                "p (g r u) -> p g r u", g=PASSES, u=2
+        def load_w(c, g):
+            w_raw = w_in.tile([P, PACK, CHUNK], BF16, name="w_raw")
+            nc.sync.dma_start(
+                out=w_raw[:],
+                in_=w_q[g * K_PASS : (g + 1) * K_PASS, c * CHUNK : (c + 1) * CHUNK].rearrange(
+                    "(p t) n -> p t n", t=PACK
+                ),
             )
+            w_raw_tiles[(c, g)] = w_raw
+
+        def turn_x(m):
+            x_words = x_raw_tiles[m][:].bitcast(F32)
             for half in range(2):
-                x_t = banks.tile([P, 2, 2, P], F32, name="x_t", tag="bank")
+                x_t = turned.tile([P, 2, 2, P], F32, name="x_t")
                 for gl in range(2):
                     for u in range(2):
                         first = (2 * half + gl) * 2 * P
@@ -101,84 +86,133 @@ def tile_mla_pb_kernel(tc, x, freqs_cos, freqs_sin, w_q, out):
                             x_words[:, first + u : first + 2 * P : 2],
                             ident[:],
                         )
+                x_turned_tiles[(m, half)] = x_t
+
+        def group_x(m):
+            x_grouped = x_stage.tile([P, PASSES * P * PACK], BF16, name="x_grouped", align_bytes=64)
+            grouped_words = x_grouped[:].bitcast(F32).rearrange(
+                "p (g r u) -> p g r u", g=PASSES, u=2
+            )
+            for half in range(2):
                 nc.scalar.copy(
                     out=grouped_words[:, 2 * half : 2 * half + 2],
-                    in_=x_t[:].rearrange("p g u r -> p g r u"),
+                    in_=x_turned_tiles[(m, half)][:].rearrange("p g u r -> p g r u"),
                 )
+            x_grouped_tiles[m] = x_grouped
+
+        def quantise_x(m):
             nc.vector.quantize_mx(
-                out=x_codes[:, m, :].bitcast(FP8X4), scales=x_scales[:, m, :], in_=x_grouped[:]
+                out=x_codes[:, m, :].bitcast(FP8X4),
+                scales=x_scales[:, m, :],
+                in_=x_grouped_tiles[m][:],
             )
 
-        def regroup_w(c, g, engine_copy):
-            w_grouped = w_stage.tile([P, CHUNK, PACK], BF16, name="w_grouped", align_bytes=64)
+        def group_w(c, g, engine_copy, first=0, last=CHUNK):
+            if (c, g) not in w_grouped_tiles:
+                w_grouped_tiles[(c, g)] = w_stage.tile(
+                    [P, CHUNK, PACK], BF16, name="w_grouped", align_bytes=64
+                )
             engine_copy(
-                out=w_grouped[:].rearrange("p (n i) t -> p n t i", i=4),
-                in_=w_raw_tiles[c][:, g].rearrange("p t (n i) -> p n t i", i=4),
+                out=w_grouped_tiles[(c, g)][:, first:last].rearrange("p (n i) t -> p n t i", i=4),
+                in_=w_raw_tiles[(c, g)][:, :, first:last].rearrange("p t (n i) -> p n t i", i=4),
             )
-            w_grouped_tiles[(c, g)] = w_grouped
 
         def quantise_w(c, g):
             nc.vector.quantize_mx(
-                out=w_code_tiles[c][:, g, :].bitcast(FP8X4),
-                scales=w_scale_tiles[c][:, g, :],
+                out=w_codes[:, c, g, :].bitcast(FP8X4),
+                scales=w_scales[:, c, g, :],
                 in_=w_grouped_tiles[(c, g)][:].rearrange("p n t -> p (n t)"),
             )
 
-        def project_and_rotate(c, m):
-            acc = banks.tile([P, CHUNK], F32, name="acc", tag="bank")
+        def project(c, m):
+            acc = sums.tile([P, CHUNK], F32, name="acc")
             for g in range(PASSES):
                 nc.tensor.matmul_mx(
                     out=acc[:],
                     lhsT=x_codes[:, m, g * P : (g + 1) * P].bitcast(FP8X4),
                     lhsT_scale=x_scales[:, m, g * P : (g + 1) * P],
-                    rhs=w_code_tiles[c][:, g, :].bitcast(FP8X4),
-                    rhs_scale=w_scale_tiles[c][:, g, :],
+                    rhs=w_codes[:, c, g, :].bitcast(FP8X4),
+                    rhs_scale=w_scales[:, c, g, :],
                     start=(g == 0),
                     stop=(g == PASSES - 1),
                 )
-            shape = [P, CHUNK_HEADS, PAIRS, 2]
-            pairs = acc[:].rearrange("p (h i e) -> p h i e", i=PAIRS, e=2)
-            t = m % SEQ_TILES
-            from_even = products.tile(shape, F32)
-            from_odd = products.tile(shape, F32)
+            return acc
+
+        def rotate(c, m, acc):
+            shape = [P, 2, CHUNK_HEADS, PAIRS, 2]
+            pairs = acc[:].rearrange("p (h i e) -> p e h i", i=PAIRS, e=2)
+            terms = products.tile(shape, F32, name="terms")
             nc.vector.tensor_tensor(
-                out=from_even[:],
-                in0=pairs[:, :, :, 0:1].to_broadcast(shape),
-                in1=table_even[:, t].unsqueeze(1).to_broadcast(shape),
+                out=terms[:],
+                in0=pairs.unsqueeze(4).to_broadcast(shape),
+                in1=table[:, m % SEQ_TILES].unsqueeze(2).to_broadcast(shape),
                 op=MULT,
             )
-            nc.vector.tensor_tensor(
-                out=from_odd[:],
-                in0=pairs[:, :, :, 1:2].to_broadcast(shape),
-                in1=table_odd[:, t].unsqueeze(1).to_broadcast(shape),
-                op=MULT,
-            )
-            rotated = results.tile(shape, F32)
-            nc.gpsimd.tensor_tensor(out=rotated[:], in0=from_even[:], in1=from_odd[:], op=ADD)
+            rotated = results.tile(shape[:1] + shape[2:], F32, name="rotated")
+            nc.gpsimd.tensor_tensor(out=rotated[:], in0=terms[:, 0], in1=terms[:, 1], op=ADD)
             nc.sync.dma_start(
                 out=out_rows[m * P : (m + 1) * P, c * CHUNK : (c + 1) * CHUNK],
                 in_=rotated[:].rearrange("p h i e -> p (h i e)"),
             )
 
-        load_x(0)
-        load_w(0)
-        for m in range(1, TOKEN_TILES):
+        for j in range(PASSES):
+            load_x(j)
+            load_w(0, j)
+        nc.scalar.dma_start(out=cos_rows[:], in_=freqs_cos.rearrange("(t p) i -> p t i", p=P))
+        nc.scalar.dma_start(out=sin_rows[:], in_=freqs_sin.rearrange("(t p) i -> p t i", p=P))
+        make_identity(nc, ident[:])
+        for m in range(PASSES, TOKEN_TILES):
             load_x(m)
-        for c in range(1, CHUNKS):
-            load_w(c)
+        later_loads = [(c, g) for c in range(1, CHUNKS) for g in range(PASSES)]
+        for c, g in later_loads[:PASSES]:
+            load_w(c, g)
+        del_loads = later_loads[PASSES:]
 
-        prepare_x(0)
-        regroup_w(0, 0, nc.vector.tensor_copy)
-        for g in range(1, PASSES):
-            regroup_w(0, g, nc.vector.tensor_copy)
-            quantise_w(0, g - 1)
-        quantise_w(0, PASSES - 1)
+        nc.vector.tensor_copy(out=table[:, :, 0, :, 0], in_=cos_rows[:])
+        nc.vector.tensor_copy(out=table[:, :, 0, :, 1], in_=sin_rows[:])
+        nc.vector.tensor_scalar_mul(out=table[:, :, 1, :, 0], in0=sin_rows[:], scalar1=-1.0)
+        nc.vector.tensor_copy(out=table[:, :, 1, :, 1], in_=cos_rows[:])
+
+        half = CHUNK // 2
+        turn_x(0)
+        group_x(0)
+        quantise_x(0)
+        turn_x(1)
+        group_w(0, 0, nc.scalar.copy)
+        group_w(0, 1, nc.vector.tensor_copy)
+        group_x(1)
+        quantise_w(0, 0)
+        quantise_w(0, 1)
+        quantise_x(1)
+        turn_x(2)
+        group_w(0, 2, nc.scalar.copy, half, CHUNK)
+        group_w(0, 2, nc.vector.tensor_copy, 0, half)
+        quantise_w(0, 2)
+        group_x(2)
+        quantise_x(2)
+        turn_x(3)
+        group_w(0, 3, nc.scalar.copy, half, CHUNK)
+        group_w(0, 3, nc.vector.tensor_copy, 0, half)
+        quantise_w(0, 3)
+        group_x(3)
+        quantise_x(3)
+        turn_x(4)
 
         for c in range(CHUNKS):
             for m in range(TOKEN_TILES):
-                if c == 0 and m + 1 < TOKEN_TILES:
-                    prepare_x(m + 1)
-                project_and_rotate(c, m)
-                if c + 1 < CHUNKS and m % 2 == 1:
-                    regroup_w(c + 1, m // 2, nc.scalar.copy)
-                    quantise_w(c + 1, m // 2)
+                acc = project(c, m)
+                if c == 0 and m + 5 < TOKEN_TILES:
+                    turn_x(m + 5)
+                rotate(c, m, acc)
+                if c == 0 and m < 4:
+                    group_x(m + 4)
+                    quantise_x(m + 4)
+                if c + 1 < CHUNKS:
+                    copies = (1, 2, 4, 5) if c == 0 else (0, 1, 2, 3)
+                    quants = (1, 3, 5, 6) if c == 0 else (0, 1, 2, 3)
+                    if m in copies:
+                        group_w(c + 1, copies.index(m), nc.scalar.copy)
+                    if m in quants:
+                        quantise_w(c + 1, quants.index(m))
+                if del_loads:
+                    load_w(*del_loads.pop(0))

@@ -38,7 +38,7 @@ def tile_mla_pb_kernel(tc, x, freqs_cos, freqs_sin, w_q, out):
         tc.tile_pool(name="w_in", bufs=CHUNKS * PASSES) as w_in,
         tc.tile_pool(name="x_stage", bufs=3) as x_stage,
         tc.tile_pool(name="w_stage", bufs=4) as w_stage,
-        tc.tile_pool(name="products", bufs=3) as products,
+        tc.tile_pool(name="products", bufs=4) as products,
         tc.tile_pool(name="results", bufs=6) as results,
         tc.psum_pool(name="turned", bufs=4) as turned,
         tc.psum_pool(name="sums", bufs=4) as sums,
@@ -148,8 +148,11 @@ def tile_mla_pb_kernel(tc, x, freqs_cos, freqs_sin, w_q, out):
                 in1=table[:, m % SEQ_TILES].unsqueeze(2).to_broadcast(shape),
                 op=MULT,
             )
-            rotated = results.tile(shape[:1] + shape[2:], F32, name="rotated")
-            nc.gpsimd.tensor_tensor(out=rotated[:], in0=terms[:, 0], in1=terms[:, 1], op=ADD)
+            return terms
+
+        def add_and_store(c, m, terms, engine_add):
+            rotated = results.tile([P, CHUNK_HEADS, PAIRS, 2], F32, name="rotated")
+            engine_add(out=rotated[:], in0=terms[:, 0], in1=terms[:, 1], op=ADD)
             nc.sync.dma_start(
                 out=out_rows[m * P : (m + 1) * P, c * CHUNK : (c + 1) * CHUNK],
                 in_=rotated[:].rearrange("p h i e -> p (h i e)"),
@@ -198,12 +201,19 @@ def tile_mla_pb_kernel(tc, x, freqs_cos, freqs_sin, w_q, out):
         quantise_x(3)
         turn_x(4)
 
+        vector_add = []
         for c in range(CHUNKS):
             for m in range(TOKEN_TILES):
                 acc = project(c, m)
                 if c == 0 and m + 5 < TOKEN_TILES:
                     turn_x(m + 5)
-                rotate(c, m, acc)
+                terms = rotate(c, m, acc)
+                if m % 4 != 3:
+                    add_and_store(c, m, terms, nc.gpsimd.tensor_tensor)
+                if m % 4 == 0 and vector_add:
+                    add_and_store(*vector_add.pop(), nc.vector.tensor_tensor)
+                if m % 4 == 3:
+                    vector_add.append((c, m, terms))
                 if c == 0 and m < 4:
                     group_x(m + 4)
                     quantise_x(m + 4)
@@ -216,3 +226,4 @@ def tile_mla_pb_kernel(tc, x, freqs_cos, freqs_sin, w_q, out):
                         quantise_w(c + 1, quants.index(m))
                 if del_loads:
                     load_w(*del_loads.pop(0))
+        add_and_store(*vector_add.pop(), nc.vector.tensor_tensor)

@@ -12,17 +12,20 @@ ADD = mybir.AluOpType.add
 P = 128
 PACK = 4
 K_PASS = P * PACK
-TOKENS = 4 * 256
+BATCHES = 4
+SEQ = 256
+TOKENS = BATCHES * SEQ
 D_IN = 2048
 D_OUT = 2048
 HEAD = 128
 PAIRS = HEAD // 2
 PASSES = D_IN // K_PASS
 TOKEN_TILES = TOKENS // P
-SEQ_TILES = 256 // P
-CHUNK = 512
+SEQ_TILES = SEQ // P
+CHUNK = 256
 CHUNKS = D_OUT // CHUNK
 CHUNK_HEADS = CHUNK // HEAD
+BLOCKS = ((0,), (1,), (2, 3), (4, 5), (6, 7))
 
 FLOPS = 2 * TOKENS * D_IN * D_OUT
 
@@ -35,9 +38,8 @@ def tile_mla_pb_kernel(tc, x, freqs_cos, freqs_sin, w_q, out):
     with (
         tc.tile_pool(name="const", bufs=1) as const,
         tc.tile_pool(name="x_in", bufs=TOKEN_TILES) as x_in,
-        tc.tile_pool(name="w_in", bufs=CHUNKS * PASSES) as w_in,
         tc.tile_pool(name="x_stage", bufs=3) as x_stage,
-        tc.tile_pool(name="w_stage", bufs=4) as w_stage,
+        tc.tile_pool(name="w_stage", bufs=5) as w_stage,
         tc.tile_pool(name="products", bufs=4) as products,
         tc.tile_pool(name="results", bufs=6) as results,
         tc.psum_pool(name="turned", bufs=4) as turned,
@@ -47,16 +49,22 @@ def tile_mla_pb_kernel(tc, x, freqs_cos, freqs_sin, w_q, out):
         ident = const.tile([P, P], F32)
         cos_rows = const.tile([P, SEQ_TILES, PAIRS], BF16)
         sin_rows = const.tile([P, SEQ_TILES, PAIRS], BF16)
-        table = const.tile([P, SEQ_TILES, 2, PAIRS, 2], BF16)
+        table = const.tile([P, 2, SEQ_TILES, PAIRS, 2], BF16)
         x_codes = const.tile([P, TOKEN_TILES, PASSES * P], U32, align_bytes=64)
         x_scales = const.tile([P, TOKEN_TILES, PASSES * P], U8, align_bytes=64)
         w_codes = const.tile([P, CHUNKS, PASSES, CHUNK], U32, align_bytes=64)
         w_scales = const.tile([P, CHUNKS, PASSES, CHUNK], U8, align_bytes=64)
+        w_raw = {}
+        for block in BLOCKS:
+            shape = [P, PASSES, PACK, len(block) * CHUNK]
+            raw = const.tile(shape, BF16, name="w_raw_%d" % block[0])
+            for i, c in enumerate(block):
+                w_raw[c] = raw[:, :, :, i * CHUNK : (i + 1) * CHUNK]
+            w_raw[block] = raw
 
         x_raw_tiles = {}
         x_turned_tiles = {}
         x_grouped_tiles = {}
-        w_raw_tiles = {}
         w_grouped_tiles = {}
 
         def load_x(m):
@@ -64,15 +72,13 @@ def tile_mla_pb_kernel(tc, x, freqs_cos, freqs_sin, w_q, out):
             nc.sync.dma_start(out=x_raw[:], in_=x_rows[m * P : (m + 1) * P, :])
             x_raw_tiles[m] = x_raw
 
-        def load_w(c, g):
-            w_raw = w_in.tile([P, PACK, CHUNK], BF16, name="w_raw")
+        def load_w(block, g):
+            rows = w_q[
+                g * K_PASS : (g + 1) * K_PASS, block[0] * CHUNK : (block[-1] + 1) * CHUNK
+            ]
             nc.sync.dma_start(
-                out=w_raw[:],
-                in_=w_q[g * K_PASS : (g + 1) * K_PASS, c * CHUNK : (c + 1) * CHUNK].rearrange(
-                    "(p t) n -> p t n", t=PACK
-                ),
+                out=w_raw[block][:, g], in_=rows.rearrange("(p t) n -> p t n", t=PACK)
             )
-            w_raw_tiles[(c, g)] = w_raw
 
         def turn_x(m):
             x_words = x_raw_tiles[m][:].bitcast(F32)
@@ -107,123 +113,129 @@ def tile_mla_pb_kernel(tc, x, freqs_cos, freqs_sin, w_q, out):
                 in_=x_grouped_tiles[m][:],
             )
 
-        def group_w(c, g, engine_copy, first=0, last=CHUNK):
-            if (c, g) not in w_grouped_tiles:
-                w_grouped_tiles[(c, g)] = w_stage.tile(
-                    [P, CHUNK, PACK], BF16, name="w_grouped", align_bytes=64
+        def group_w(c, g, engine_copy):
+            if (c, g // 2) not in w_grouped_tiles:
+                w_grouped_tiles[(c, g // 2)] = w_stage.tile(
+                    [P, 2, CHUNK, PACK], BF16, name="w_grouped", align_bytes=64
                 )
             engine_copy(
-                out=w_grouped_tiles[(c, g)][:, first:last].rearrange("p (n i) t -> p n t i", i=4),
-                in_=w_raw_tiles[(c, g)][:, :, first:last].rearrange("p t (n i) -> p n t i", i=4),
+                out=w_grouped_tiles[(c, g // 2)][:, g % 2].rearrange("p (n i) t -> p n t i", i=4),
+                in_=w_raw[c][:, g].rearrange("p t (n i) -> p n t i", i=4),
             )
 
-        def quantise_w(c, g):
+        def quantise_w(c, half):
+            passes = slice(2 * half, 2 * half + 2)
             nc.vector.quantize_mx(
-                out=w_codes[:, c, g, :].bitcast(FP8X4),
-                scales=w_scales[:, c, g, :],
-                in_=w_grouped_tiles[(c, g)][:].rearrange("p n t -> p (n t)"),
+                out=w_codes[:, c, passes, :].rearrange("p g n -> p (g n)").bitcast(FP8X4),
+                scales=w_scales[:, c, passes, :].rearrange("p g n -> p (g n)"),
+                in_=w_grouped_tiles[(c, half)][:].rearrange("p g n t -> p (g n t)"),
             )
 
-        def project(c, m):
-            acc = sums.tile([P, CHUNK], F32, name="acc")
-            for g in range(PASSES):
-                nc.tensor.matmul_mx(
-                    out=acc[:],
-                    lhsT=x_codes[:, m, g * P : (g + 1) * P].bitcast(FP8X4),
-                    lhsT_scale=x_scales[:, m, g * P : (g + 1) * P],
-                    rhs=w_codes[:, c, g, :].bitcast(FP8X4),
-                    rhs_scale=w_scales[:, c, g, :],
-                    start=(g == 0),
-                    stop=(g == PASSES - 1),
-                )
+        def project(c, b):
+            acc = sums.tile([P, SEQ_TILES, CHUNK], F32, name="acc")
+            for t in range(SEQ_TILES):
+                m = b * SEQ_TILES + t
+                for g in range(PASSES):
+                    nc.tensor.matmul_mx(
+                        out=acc[:, t, :],
+                        lhsT=x_codes[:, m, g * P : (g + 1) * P].bitcast(FP8X4),
+                        lhsT_scale=x_scales[:, m, g * P : (g + 1) * P],
+                        rhs=w_codes[:, c, g, :].bitcast(FP8X4),
+                        rhs_scale=w_scales[:, c, g, :],
+                        start=(g == 0),
+                        stop=(g == PASSES - 1),
+                    )
             return acc
 
-        def rotate(c, m, acc):
-            shape = [P, 2, CHUNK_HEADS, PAIRS, 2]
-            pairs = acc[:].rearrange("p (h i e) -> p e h i", i=PAIRS, e=2)
+        def rotate(acc):
+            shape = [P, 2, SEQ_TILES, CHUNK_HEADS, PAIRS, 2]
+            pairs = acc[:].rearrange("p t (h i e) -> p e t h i", i=PAIRS, e=2)
             terms = products.tile(shape, F32, name="terms")
             nc.vector.tensor_tensor(
                 out=terms[:],
-                in0=pairs.unsqueeze(4).to_broadcast(shape),
-                in1=table[:, m % SEQ_TILES].unsqueeze(2).to_broadcast(shape),
+                in0=pairs.unsqueeze(5).to_broadcast(shape),
+                in1=table[:].unsqueeze(3).to_broadcast(shape),
                 op=MULT,
             )
             return terms
 
-        def add_and_store(c, m, terms, engine_add):
-            rotated = results.tile([P, CHUNK_HEADS, PAIRS, 2], F32, name="rotated")
+        def add_and_store(c, b, terms, engine_add):
+            rotated = results.tile([P, SEQ_TILES, CHUNK_HEADS, PAIRS, 2], F32, name="rotated")
             engine_add(out=rotated[:], in0=terms[:, 0], in1=terms[:, 1], op=ADD)
+            rows = out_rows[b * SEQ : (b + 1) * SEQ, c * CHUNK : (c + 1) * CHUNK]
             nc.sync.dma_start(
-                out=out_rows[m * P : (m + 1) * P, c * CHUNK : (c + 1) * CHUNK],
-                in_=rotated[:].rearrange("p h i e -> p (h i e)"),
+                out=rows.rearrange("(t p) n -> p t n", p=P),
+                in_=rotated[:].rearrange("p t h i e -> p t (h i e)"),
             )
 
         for j in range(PASSES):
             load_x(j)
-            load_w(0, j)
+            load_w(BLOCKS[0], j)
         nc.scalar.dma_start(out=cos_rows[:], in_=freqs_cos.rearrange("(t p) i -> p t i", p=P))
         nc.scalar.dma_start(out=sin_rows[:], in_=freqs_sin.rearrange("(t p) i -> p t i", p=P))
         make_identity(nc, ident[:])
+        for g in range(PASSES):
+            load_w(BLOCKS[1], g)
         for m in range(PASSES, TOKEN_TILES):
             load_x(m)
-        later_loads = [(c, g) for c in range(1, CHUNKS) for g in range(PASSES)]
-        for c, g in later_loads[:PASSES]:
-            load_w(c, g)
-        del_loads = later_loads[PASSES:]
+        later_loads = [(block, g) for block in BLOCKS[2:] for g in range(PASSES)]
+        for block, g in later_loads[:PASSES]:
+            load_w(block, g)
+        later_loads = later_loads[PASSES:]
 
-        nc.vector.tensor_copy(out=table[:, :, 0, :, 0], in_=cos_rows[:])
-        nc.vector.tensor_copy(out=table[:, :, 0, :, 1], in_=sin_rows[:])
-        nc.vector.tensor_scalar_mul(out=table[:, :, 1, :, 0], in0=sin_rows[:], scalar1=-1.0)
-        nc.vector.tensor_copy(out=table[:, :, 1, :, 1], in_=cos_rows[:])
+        nc.vector.tensor_copy(out=table[:, 0, :, :, 0], in_=cos_rows[:])
+        nc.vector.tensor_copy(out=table[:, 0, :, :, 1], in_=sin_rows[:])
+        nc.vector.tensor_scalar_mul(out=table[:, 1, :, :, 0], in0=sin_rows[:], scalar1=-1.0)
+        nc.vector.tensor_copy(out=table[:, 1, :, :, 1], in_=cos_rows[:])
 
-        half = CHUNK // 2
         turn_x(0)
         group_x(0)
         quantise_x(0)
-        turn_x(1)
         group_w(0, 0, nc.scalar.copy)
         group_w(0, 1, nc.vector.tensor_copy)
-        group_x(1)
         quantise_w(0, 0)
-        quantise_w(0, 1)
+        turn_x(1)
+        group_x(1)
         quantise_x(1)
         turn_x(2)
-        group_w(0, 2, nc.scalar.copy, half, CHUNK)
-        group_w(0, 2, nc.vector.tensor_copy, 0, half)
-        quantise_w(0, 2)
         group_x(2)
+        group_w(0, 2, nc.scalar.copy)
+        group_w(0, 3, nc.vector.tensor_copy)
         quantise_x(2)
+        quantise_w(0, 1)
         turn_x(3)
-        group_w(0, 3, nc.scalar.copy, half, CHUNK)
-        group_w(0, 3, nc.vector.tensor_copy, 0, half)
-        quantise_w(0, 3)
         group_x(3)
         quantise_x(3)
-        turn_x(4)
+        for g in range(PASSES):
+            group_w(1, g, nc.scalar.copy)
 
-        vector_add = []
-        for c in range(CHUNKS):
-            for m in range(TOKEN_TILES):
-                acc = project(c, m)
-                if c == 0 and m + 5 < TOKEN_TILES:
-                    turn_x(m + 5)
-                terms = rotate(c, m, acc)
-                if m % 4 != 3:
-                    add_and_store(c, m, terms, nc.gpsimd.tensor_tensor)
-                if m % 4 == 0 and vector_add:
-                    add_and_store(*vector_add.pop(), nc.vector.tensor_tensor)
-                if m % 4 == 3:
-                    vector_add.append((c, m, terms))
-                if c == 0 and m < 4:
-                    group_x(m + 4)
-                    quantise_x(m + 4)
-                if c + 1 < CHUNKS:
-                    copies = (1, 2, 4, 5) if c == 0 else (0, 1, 2, 3)
-                    quants = (1, 3, 5, 6) if c == 0 else (0, 1, 2, 3)
-                    if m in copies:
-                        group_w(c + 1, copies.index(m), nc.scalar.copy)
-                    if m in quants:
-                        quantise_w(c + 1, quants.index(m))
-                if del_loads:
-                    load_w(*del_loads.pop(0))
-        add_and_store(*vector_add.pop(), nc.vector.tensor_tensor)
+        units = [(0, 0), (0, 1), (1, 0), (1, 1), (0, 2), (1, 2), (0, 3), (1, 3)]
+        units += [(c, b) for c in range(2, CHUNKS) for b in range(BATCHES)]
+        turn_after = {1: (4, 5), 2: (6,), 3: (7,)}
+        quantise_x_after = {2: (4,), 3: (5, 6, 7)}
+        waiting = []
+        for u, (c, b) in enumerate(units):
+            acc = project(c, b)
+            for m in turn_after.get(u, ()):
+                turn_x(m)
+                group_x(m)
+            terms = rotate(acc)
+            while waiting:
+                add_and_store(*waiting.pop(), nc.vector.tensor_tensor)
+            if (u % 4 == 0 and u > 0) or u == len(units) - 1:
+                waiting.append((c, b, terms))
+            else:
+                add_and_store(c, b, terms, nc.gpsimd.tensor_tensor)
+            if u == 1:
+                quantise_w(1, 0)
+                quantise_w(1, 1)
+            for m in quantise_x_after.get(u, ()):
+                quantise_x(m)
+            if u % 4 == 1 and u > 1 and u // 4 + 1 < CHUNKS:
+                for g in range(PASSES):
+                    group_w(u // 4 + 1, g, nc.scalar.copy)
+                quantise_w(u // 4 + 1, 0)
+                quantise_w(u // 4 + 1, 1)
+            if later_loads:
+                load_w(*later_loads.pop(0))
+        add_and_store(*waiting.pop(), nc.vector.tensor_tensor)

@@ -39,7 +39,7 @@ def tile_mla_pb_kernel(tc, x, freqs_cos, freqs_sin, w_q, out):
         tc.tile_pool(name="const", bufs=1) as const,
         tc.tile_pool(name="x_in", bufs=TOKEN_TILES) as x_in,
         tc.tile_pool(name="x_stage", bufs=3) as x_stage,
-        tc.tile_pool(name="w_stage", bufs=5) as w_stage,
+        tc.tile_pool(name="w_stage", bufs=3) as w_stage,
         tc.tile_pool(name="products", bufs=4) as products,
         tc.tile_pool(name="results", bufs=6) as results,
         tc.psum_pool(name="turned", bufs=4) as turned,
@@ -114,21 +114,21 @@ def tile_mla_pb_kernel(tc, x, freqs_cos, freqs_sin, w_q, out):
             )
 
         def group_w(c, g, engine_copy):
-            if (c, g // 2) not in w_grouped_tiles:
-                w_grouped_tiles[(c, g // 2)] = w_stage.tile(
-                    [P, 2, CHUNK, PACK], BF16, name="w_grouped", align_bytes=64
+            if c not in w_grouped_tiles:
+                w_grouped_tiles[c] = w_stage.tile(
+                    [P, PASSES, CHUNK, PACK], BF16, name="w_grouped", align_bytes=64
                 )
             engine_copy(
-                out=w_grouped_tiles[(c, g // 2)][:, g % 2].rearrange("p (n i) t -> p n t i", i=4),
+                out=w_grouped_tiles[c][:, g].rearrange("p (n i) t -> p n t i", i=4),
                 in_=w_raw[c][:, g].rearrange("p t (n i) -> p n t i", i=4),
             )
 
-        def quantise_w(c, half):
-            passes = slice(2 * half, 2 * half + 2)
+        def quantise_w(c, first, last):
+            passes = slice(first, last)
             nc.vector.quantize_mx(
                 out=w_codes[:, c, passes, :].rearrange("p g n -> p (g n)").bitcast(FP8X4),
                 scales=w_scales[:, c, passes, :].rearrange("p g n -> p (g n)"),
-                in_=w_grouped_tiles[(c, half)][:].rearrange("p g n t -> p (g n t)"),
+                in_=w_grouped_tiles[c][:, passes].rearrange("p g n t -> p (g n t)"),
             )
 
         def project(c, b):
@@ -159,18 +159,26 @@ def tile_mla_pb_kernel(tc, x, freqs_cos, freqs_sin, w_q, out):
             )
             return terms
 
-        def add_and_store(c, b, terms, engine_add):
-            rotated = results.tile([P, SEQ_TILES, CHUNK_HEADS, PAIRS, 2], F32, name="rotated")
-            engine_add(out=rotated[:], in0=terms[:, 0], in1=terms[:, 1], op=ADD)
+        def add(terms, engine_add):
+            rotated = results.tile([P, SEQ_TILES, CHUNK], F32, name="rotated")
+            even, odd = (terms[:, e].rearrange("p t h i e -> p t (h i e)") for e in range(2))
+            engine_add(out=rotated[:], in0=even, in1=odd, op=ADD)
+            return rotated
+
+        def store(c, b, rotated):
             rows = out_rows[b * SEQ : (b + 1) * SEQ, c * CHUNK : (c + 1) * CHUNK]
             nc.sync.dma_start(
-                out=rows.rearrange("(t p) n -> p t n", p=P),
-                in_=rotated[:].rearrange("p t h i e -> p t (h i e)"),
+                out=rows.rearrange("(t p) n -> p t n", p=P), in_=rotated[:]
             )
 
-        for j in range(PASSES):
-            load_x(j)
-            load_w(BLOCKS[0], j)
+        load_w(BLOCKS[0], 0)
+        load_w(BLOCKS[0], 1)
+        load_x(0)
+        load_w(BLOCKS[0], 2)
+        load_x(1)
+        load_w(BLOCKS[0], 3)
+        load_x(2)
+        load_x(3)
         nc.scalar.dma_start(out=cos_rows[:], in_=freqs_cos.rearrange("(t p) i -> p t i", p=P))
         nc.scalar.dma_start(out=sin_rows[:], in_=freqs_sin.rearrange("(t p) i -> p t i", p=P))
         make_identity(nc, ident[:])
@@ -183,59 +191,84 @@ def tile_mla_pb_kernel(tc, x, freqs_cos, freqs_sin, w_q, out):
             load_w(block, g)
         later_loads = later_loads[PASSES:]
 
-        nc.vector.tensor_copy(out=table[:, 0, :, :, 0], in_=cos_rows[:])
-        nc.vector.tensor_copy(out=table[:, 0, :, :, 1], in_=sin_rows[:])
-        nc.vector.tensor_scalar_mul(out=table[:, 1, :, :, 0], in0=sin_rows[:], scalar1=-1.0)
-        nc.vector.tensor_copy(out=table[:, 1, :, :, 1], in_=cos_rows[:])
+        zeros = const.tile([P, 512], BF16)
+        nc.gpsimd.memset(zeros[:], 0.0)
 
+        def keep_warm(count):
+            for i in range(count):
+                unread = sums.tile([P, 512], F32, name="acc")
+                nc.tensor.matmul(
+                    unread[:], lhsT=zeros[:, :P], rhs=zeros[:], start=True, stop=True
+                )
+
+        nc.gpsimd.tensor_copy(out=table[:, 0, :, :, 0], in_=cos_rows[:])
+        nc.gpsimd.tensor_copy(out=table[:, 0, :, :, 1], in_=sin_rows[:])
+        nc.gpsimd.tensor_scalar_mul(out=table[:, 1, :, :, 0], in0=sin_rows[:], scalar1=-1.0)
+        nc.gpsimd.tensor_copy(out=table[:, 1, :, :, 1], in_=cos_rows[:])
+        keep_warm(4)
+
+        group_w(0, 0, nc.vector.tensor_copy)
+        group_w(0, 1, nc.vector.tensor_copy)
+        quantise_w(0, 0, 2)
         turn_x(0)
         group_x(0)
+        group_w(0, 2, nc.vector.tensor_copy)
         quantise_x(0)
-        group_w(0, 0, nc.scalar.copy)
-        group_w(0, 1, nc.vector.tensor_copy)
-        quantise_w(0, 0)
+        keep_warm(2)
         turn_x(1)
         group_x(1)
+        group_w(0, 3, nc.vector.tensor_copy)
+        quantise_w(0, 2, 4)
         quantise_x(1)
+        keep_warm(1)
         turn_x(2)
         group_x(2)
-        group_w(0, 2, nc.scalar.copy)
-        group_w(0, 3, nc.vector.tensor_copy)
-        quantise_x(2)
-        quantise_w(0, 1)
         turn_x(3)
         group_x(3)
-        quantise_x(3)
-        for g in range(PASSES):
+        for g in range(PASSES - 1):
             group_w(1, g, nc.scalar.copy)
+        quantise_x(2)
+        quantise_x(3)
 
         units = [(0, 0), (0, 1), (1, 0), (1, 1), (0, 2), (1, 2), (0, 3), (1, 3)]
         units += [(c, b) for c in range(2, CHUNKS) for b in range(BATCHES)]
-        turn_after = {1: (4, 5), 2: (6,), 3: (7,)}
-        quantise_x_after = {2: (4,), 3: (5, 6, 7)}
-        waiting = []
+        turn_after = {1: (4, 5, 6), 3: (7,)}
+        quantise_x_after = {1: (4, 5), 3: (6, 7)}
+        last = len(units) - 1
+        on_vector = {u: u + 1 for u in range(4, last, 4)}
+        on_vector[last] = last + 1
+        kept = {}
         for u, (c, b) in enumerate(units):
             acc = project(c, b)
             for m in turn_after.get(u, ()):
                 turn_x(m)
                 group_x(m)
-            terms = rotate(acc)
-            while waiting:
-                add_and_store(*waiting.pop(), nc.vector.tensor_tensor)
-            if (u % 4 == 0 and u > 0) or u == len(units) - 1:
-                waiting.append((c, b, terms))
-            else:
-                add_and_store(c, b, terms, nc.gpsimd.tensor_tensor)
+            kept[u] = rotate(acc)
+            for v in on_vector:
+                if on_vector[v] == u:
+                    store(*units[v], add(kept[v], nc.vector.tensor_tensor))
+            if u not in on_vector:
+                store(c, b, add(kept[u], nc.gpsimd.tensor_tensor))
+            if u == 0:
+                group_w(1, PASSES - 1, nc.vector.tensor_copy)
             if u == 1:
-                quantise_w(1, 0)
-                quantise_w(1, 1)
+                quantise_w(1, 0, 2)
+                quantise_w(1, 2, 4)
             for m in quantise_x_after.get(u, ()):
                 quantise_x(m)
-            if u % 4 == 1 and u > 1 and u // 4 + 1 < CHUNKS:
+            if u == 3:
                 for g in range(PASSES):
-                    group_w(u // 4 + 1, g, nc.scalar.copy)
-                quantise_w(u // 4 + 1, 0)
-                quantise_w(u // 4 + 1, 1)
+                    group_w(2, g, nc.scalar.copy)
+            if u % 4 == 1 and u > 1:
+                if u // 4 + 1 < CHUNKS:
+                    if u // 4 + 1 < 4:
+                        quantise_w(u // 4 + 1, 0, 2)
+                        quantise_w(u // 4 + 1, 2, 4)
+                    else:
+                        quantise_w(u // 4 + 1, 0, 4)
+                if u // 4 + 2 < CHUNKS:
+                    for g in range(PASSES):
+                        group_w(u // 4 + 2, g, nc.scalar.copy)
             if later_loads:
                 load_w(*later_loads.pop(0))
-        add_and_store(*waiting.pop(), nc.vector.tensor_tensor)
+        store(*units[last], add(kept[last], nc.vector.tensor_tensor))

@@ -232,10 +232,10 @@ def tile_mla_pb_kernel(tc, x, freqs_cos, freqs_sin, w_q, out):
 
         units = [(0, 0), (0, 1), (1, 0), (1, 1), (0, 2), (1, 2), (0, 3), (1, 3)]
         units += [(c, b) for c in range(2, CHUNKS) for b in range(BATCHES)]
-        turn_after = {1: (4, 5, 6), 3: (7,)}
-        quantise_x_after = {1: (4, 5), 3: (6, 7)}
+        turn_after = {1: (4, 5, 6), 2: (7,)}
+        quantise_x_after = {1: (4, 5), 2: (6,), 3: (7,)}
         last = len(units) - 1
-        on_vector = {u: u + 1 for u in range(4, last, 4)}
+        on_vector = {u: u + 1 for u in range(8, last, 4)}
         on_vector[last] = last + 1
         kept = {}
         for u, (c, b) in enumerate(units):

import concourse.mybir as mybir
from concourse.masks import make_identity

F32 = mybir.dt.float32
BF16 = mybir.dt.bfloat16
U32 = mybir.dt.uint32
U8 = mybir.dt.uint8
FP8X4 = mybir.dt.float8_e4m3fn_x4
MULT = mybir.AluOpType.mult
ADD = mybir.AluOpType.add

P = 128
PACK = 4
K_PASS = P * PACK
BATCHES = 4
SEQ = 256
TOKENS = BATCHES * SEQ
D_IN = 2048
D_OUT = 2048
HEAD = 128
PAIRS = HEAD // 2
PASSES = D_IN // K_PASS
TOKEN_TILES = TOKENS // P
SEQ_TILES = SEQ // P
CHUNK = 256
CHUNKS = D_OUT // CHUNK
CHUNK_HEADS = CHUNK // HEAD
BLOCKS = ((0,), (1,), (2, 3), (4, 5), (6, 7))

FLOPS = 2 * TOKENS * D_IN * D_OUT


def tile_mla_pb_kernel(tc, x, freqs_cos, freqs_sin, w_q, out):
    nc = tc.nc
    x_rows = x.flatten_outer_dims()
    out_rows = out.rearrange("b s h d -> (b s) (h d)")

    with (
        tc.tile_pool(name="const", bufs=1) as const,
        tc.tile_pool(name="x_in", bufs=TOKEN_TILES) as x_in,
        tc.tile_pool(name="x_stage", bufs=3) as x_stage,
        tc.tile_pool(name="w_stage", bufs=3) as w_stage,
        tc.tile_pool(name="products", bufs=4) as products,
        tc.tile_pool(name="results", bufs=6) as results,
        tc.psum_pool(name="turned", bufs=4) as turned,
        tc.psum_pool(name="sums", bufs=4) as sums,
        tc.manual_schedule(),
    ):
        ident = const.tile([P, P], F32)
        cos_rows = const.tile([P, SEQ_TILES, PAIRS], BF16)
        sin_rows = const.tile([P, SEQ_TILES, PAIRS], BF16)
        table = const.tile([P, 2, SEQ_TILES, PAIRS, 2], BF16)
        x_codes = const.tile([P, TOKEN_TILES, PASSES * P], U32, align_bytes=64)
        x_scales = const.tile([P, TOKEN_TILES, PASSES * P], U8, align_bytes=64)
        w_codes = const.tile([P, CHUNKS, PASSES, CHUNK], U32, align_bytes=64)
        w_scales = const.tile([P, CHUNKS, PASSES, CHUNK], U8, align_bytes=64)
        w_raw = {}
        for block in BLOCKS:
            shape = [P, PASSES, PACK, len(block) * CHUNK]
            raw = const.tile(shape, BF16, name="w_raw_%d" % block[0])
            for i, c in enumerate(block):
                w_raw[c] = raw[:, :, :, i * CHUNK : (i + 1) * CHUNK]
            w_raw[block] = raw

        x_raw_tiles = {}
        x_turned_tiles = {}
        x_grouped_tiles = {}
        w_grouped_tiles = {}

        def load_x(m):
            x_raw = x_in.tile([P, D_IN], BF16, name="x_raw")
            nc.sync.dma_start(out=x_raw[:], in_=x_rows[m * P : (m + 1) * P, :])
            x_raw_tiles[m] = x_raw

        def load_w(block, g):
            rows = w_q[
                g * K_PASS : (g + 1) * K_PASS, block[0] * CHUNK : (block[-1] + 1) * CHUNK
            ]
            nc.sync.dma_start(
                out=w_raw[block][:, g], in_=rows.rearrange("(p t) n -> p t n", t=PACK)
            )

        def turn_x(m):
            x_words = x_raw_tiles[m][:].bitcast(F32)
            for half in range(2):
                x_t = turned.tile([P, 2, 2, P], F32, name="x_t")
                for gl in range(2):
                    for u in range(2):
                        first = (2 * half + gl) * 2 * P
                        nc.tensor.transpose(
                            x_t[:, gl, u, :],
                            x_words[:, first + u : first + 2 * P : 2],
                            ident[:],
                        )
                x_turned_tiles[(m, half)] = x_t

        def group_x(m):
            x_grouped = x_stage.tile([P, PASSES * P * PACK], BF16, name="x_grouped", align_bytes=64)
            grouped_words = x_grouped[:].bitcast(F32).rearrange(
                "p (g r u) -> p g r u", g=PASSES, u=2
            )
            for half in range(2):
                nc.scalar.copy(
                    out=grouped_words[:, 2 * half : 2 * half + 2],
                    in_=x_turned_tiles[(m, half)][:].rearrange("p g u r -> p g r u"),
                )
            x_grouped_tiles[m] = x_grouped

        def quantise_x(m):
            nc.vector.quantize_mx(
                out=x_codes[:, m, :].bitcast(FP8X4),
                scales=x_scales[:, m, :],
                in_=x_grouped_tiles[m][:],
            )

        def group_w(c, g, engine_copy):
            if c not in w_grouped_tiles:
                w_grouped_tiles[c] = w_stage.tile(
                    [P, PASSES, CHUNK, PACK], BF16, name="w_grouped", align_bytes=64
                )
            engine_copy(
                out=w_grouped_tiles[c][:, g].rearrange("p (n i) t -> p n t i", i=4),
                in_=w_raw[c][:, g].rearrange("p t (n i) -> p n t i", i=4),
            )

        def quantise_w(c, first, last):
            passes = slice(first, last)
            nc.vector.quantize_mx(
                out=w_codes[:, c, passes, :].rearrange("p g n -> p (g n)").bitcast(FP8X4),
                scales=w_scales[:, c, passes, :].rearrange("p g n -> p (g n)"),
                in_=w_grouped_tiles[c][:, passes].rearrange("p g n t -> p (g n t)"),
            )

        def project(c, b):
            acc = sums.tile([P, SEQ_TILES, CHUNK], F32, name="acc")
            for t in range(SEQ_TILES):
                m = b * SEQ_TILES + t
                for g in range(PASSES):
                    nc.tensor.matmul_mx(
                        out=acc[:, t, :],
                        lhsT=x_codes[:, m, g * P : (g + 1) * P].bitcast(FP8X4),
                        lhsT_scale=x_scales[:, m, g * P : (g + 1) * P],
                        rhs=w_codes[:, c, g, :].bitcast(FP8X4),
                        rhs_scale=w_scales[:, c, g, :],
                        start=(g == 0),
                        stop=(g == PASSES - 1),
                    )
            return acc

        def rotate(acc):
            shape = [P, 2, SEQ_TILES, CHUNK_HEADS, PAIRS, 2]
            pairs = acc[:].rearrange("p t (h i e) -> p e t h i", i=PAIRS, e=2)
            terms = products.tile(shape, F32, name="terms")
            nc.vector.tensor_tensor(
                out=terms[:],
                in0=pairs.unsqueeze(5).to_broadcast(shape),
                in1=table[:].unsqueeze(3).to_broadcast(shape),
                op=MULT,
            )
            return terms

        def add(terms, engine_add):
            rotated = results.tile([P, SEQ_TILES, CHUNK], F32, name="rotated")
            even, odd = (terms[:, e].rearrange("p t h i e -> p t (h i e)") for e in range(2))
            engine_add(out=rotated[:], in0=even, in1=odd, op=ADD)
            return rotated

        def store(c, b, rotated):
            rows = out_rows[b * SEQ : (b + 1) * SEQ, c * CHUNK : (c + 1) * CHUNK]
            nc.sync.dma_start(
                out=rows.rearrange("(t p) n -> p t n", p=P), in_=rotated[:]
            )

        load_w(BLOCKS[0], 0)
        load_w(BLOCKS[0], 1)
        load_x(0)
        load_w(BLOCKS[0], 2)
        load_x(1)
        load_w(BLOCKS[0], 3)
        load_x(2)
        load_x(3)
        nc.scalar.dma_start(out=cos_rows[:], in_=freqs_cos.rearrange("(t p) i -> p t i", p=P))
        nc.scalar.dma_start(out=sin_rows[:], in_=freqs_sin.rearrange("(t p) i -> p t i", p=P))
        make_identity(nc, ident[:])
        for g in range(PASSES):
            load_w(BLOCKS[1], g)
        for m in range(PASSES, TOKEN_TILES):
            load_x(m)
        later_loads = [(block, g) for block in BLOCKS[2:] for g in range(PASSES)]
        for block, g in later_loads[:PASSES]:
            load_w(block, g)
        later_loads = later_loads[PASSES:]

        zeros = const.tile([P, 512], BF16)
        nc.gpsimd.memset(zeros[:], 0.0)

        def keep_warm(count):
            for i in range(count):
                unread = sums.tile([P, 512], F32, name="acc")
                nc.tensor.matmul(
                    unread[:], lhsT=zeros[:, :P], rhs=zeros[:], start=True, stop=True
                )

        nc.gpsimd.tensor_copy(out=table[:, 0, :, :, 0], in_=cos_rows[:])
        nc.gpsimd.tensor_copy(out=table[:, 0, :, :, 1], in_=sin_rows[:])
        nc.gpsimd.tensor_scalar_mul(out=table[:, 1, :, :, 0], in0=sin_rows[:], scalar1=-1.0)
        nc.gpsimd.tensor_copy(out=table[:, 1, :, :, 1], in_=cos_rows[:])
        keep_warm(4)

        group_w(0, 0, nc.vector.tensor_copy)
        group_w(0, 1, nc.vector.tensor_copy)
        quantise_w(0, 0, 2)
        turn_x(0)
        group_x(0)
        group_w(0, 2, nc.vector.tensor_copy)
        quantise_x(0)
        keep_warm(2)
        turn_x(1)
        group_x(1)
        group_w(0, 3, nc.vector.tensor_copy)
        quantise_w(0, 2, 4)
        quantise_x(1)
        keep_warm(1)
        turn_x(2)
        group_x(2)
        turn_x(3)
        group_x(3)
        for g in range(PASSES - 1):
            group_w(1, g, nc.scalar.copy)
        quantise_x(2)
        quantise_x(3)

        units = [(0, 0), (0, 1), (1, 0), (1, 1), (0, 2), (1, 2), (0, 3), (1, 3)]
        units += [(c, b) for c in range(2, CHUNKS) for b in range(BATCHES)]
        turn_after = {1: (4, 5, 6), 2: (7,)}
        quantise_x_after = {1: (4, 5), 2: (6,), 3: (7,)}
        last = len(units) - 1
        on_vector = {u: u + 1 for u in range(8, last, 4)}
        on_vector[last] = last + 1
        kept = {}
        for u, (c, b) in enumerate(units):
            acc = project(c, b)
            for m in turn_after.get(u, ()):
                turn_x(m)
                group_x(m)
            kept[u] = rotate(acc)
            for v in on_vector:
                if on_vector[v] == u:
                    store(*units[v], add(kept[v], nc.vector.tensor_tensor))
            if u not in on_vector:
                store(c, b, add(kept[u], nc.gpsimd.tensor_tensor))
            if u == 0:
                group_w(1, PASSES - 1, nc.vector.tensor_copy)
            if u == 1:
                quantise_w(1, 0, 2)
                quantise_w(1, 2, 4)
            for m in quantise_x_after.get(u, ()):
                quantise_x(m)
            if u == 3:
                for g in range(PASSES):
                    group_w(2, g, nc.scalar.copy)
            if u % 4 == 1 and u > 1:
                if u // 4 + 1 < CHUNKS:
                    if u // 4 + 1 < 4:
                        quantise_w(u // 4 + 1, 0, 2)
                        quantise_w(u // 4 + 1, 2, 4)
                    else:
                        quantise_w(u // 4 + 1, 0, 4)
                if u // 4 + 2 < CHUNKS:
                    for g in range(PASSES):
                        group_w(u // 4 + 2, g, nc.scalar.copy)
            if later_loads:
                load_w(*later_loads.pop(0))
        store(*units[last], add(kept[last], nc.vector.tensor_tensor))
